import numpy as np
import ml_dtypes


def mxq(x, axis, fmt="e4m3"):
    dtype, down = {"e4m3": (ml_dtypes.float8_e4m3fn, 7), "e5m2": (ml_dtypes.float8_e5m2, 14)}[fmt]
    v = np.moveaxis(np.asarray(x, np.float32).astype(ml_dtypes.bfloat16).astype(np.float64), axis, -1)
    blocks = v.reshape(v.shape[:-1] + (-1, 32))
    amax = np.abs(blocks).max(-1, keepdims=True)
    byte = np.maximum(np.where(amax > 0, np.frexp(amax)[1] - 1 + 127, 0) - down, 1)
    scale = np.exp2(byte - 127.0)
    codes = (blocks / scale).astype(np.float32).astype(dtype).astype(np.float64)
    return np.moveaxis((codes * scale).reshape(v.shape), -1, axis)


WIDE = False


def mx_kscale(k):
    if not WIDE:
        return np.ones(k)
    levels = np.array([10, -10, 5, -5, 0])
    a = np.random.permutation(np.resize(levels, k // 512 * 4)).reshape(k // 512, 4)
    idx = np.arange(k)
    return np.exp2(a[idx // 512, idx % 128 // 32])


BF16 = ml_dtypes.bfloat16


def bf(x):
    return np.asarray(x, np.float32).astype(BF16)


def f64(x):
    return np.asarray(x).astype(np.float64)


E2M1 = np.array([0.0, 0.5, 1.0, 1.5, 2.0, 3.0, 4.0, 6.0, -0.0, -0.5, -1.0, -1.5, -2.0, -3.0, -4.0, -6.0])


def pack_weight(w, fmt):
    k, n = w.shape
    w = f64(bf(w)).reshape(k // 32, 32, n)
    amax = np.abs(w).max(1)
    if fmt == "e4m3":
        byte = np.frexp(amax)[1] - 1 + 127 - 7
    else:
        mant, ex = np.frexp(amax / 6.0)
        byte = np.where(mant > 0.5, ex, ex - 1) + 127
    byte = np.clip(np.where(amax > 0, byte, 1), 1, 254)
    scaled = (w * np.exp2(127.0 - byte)[:, None, :]).reshape(k, n).astype(np.float32)
    by_word = np.ascontiguousarray(scaled.reshape(k // 512, 128, 4, n).transpose(0, 1, 3, 2))
    if fmt == "e4m3":
        words = by_word.astype(ml_dtypes.float8_e4m3fn).view(np.uint8)
    else:
        c = by_word.astype(ml_dtypes.float4_e2m1fn).view(np.uint8) & 0xF
        words = c[..., 0::2] | (c[..., 1::2] << 4)
    return np.ascontiguousarray(words), np.ascontiguousarray(byte.astype(np.uint8).reshape(k // 512, 16, n))


def unpack_weight(words, scales, fmt):
    g, p, n, _ = words.shape
    if fmt == "e4m3":
        vals = np.ascontiguousarray(words).view(ml_dtypes.float8_e4m3fn).astype(np.float64)
    else:
        nib = np.empty((g, p, n, 4), np.uint8)
        nib[..., 0::2] = words & 0xF
        nib[..., 1::2] = words >> 4
        vals = E2M1[nib]
    vals = vals * np.repeat(np.exp2(scales.astype(np.float64) - 127.0), 8, axis=1)[..., None]
    return vals.transpose(0, 1, 3, 2).reshape(g * 512, n)


B, P_DIM, H_DIM, X_DIM = 128, 8192, 512, 2048
FMT = "e4m3"


def sigmoid(v):
    return 1.0 / (1.0 + np.exp(-v))


def setup_inputs():
    sp, sh, sx = mx_kscale(P_DIM), mx_kscale(H_DIM), mx_kscale(X_DIM)

    def lin_w(in_d, s):
        w = np.random.standard_normal((H_DIM, in_d)) * 0.6 / np.sqrt(in_d) / s[None, :]
        return pack_weight(np.ascontiguousarray(w.T), FMT)

    def lin_b():
        return bf(np.random.standard_normal(H_DIM) * 0.5)

    out = {
        "P": bf(np.random.standard_normal((B, P_DIM)) * sp),
        "hidden": bf(np.random.standard_normal((B, H_DIM)) * sh),
        "cell": bf(np.random.standard_normal((B, H_DIM))),
        "ext_input": bf(np.random.standard_normal((B, X_DIM)) * sx),
    }
    for k in "ifgo":
        out["W_p" + k + "_words"], out["W_p" + k + "_scales"] = lin_w(P_DIM, sp)
        out["b_p" + k] = lin_b()
    for k in "ifgo":
        out["W_h" + k + "_words"], out["W_h" + k + "_scales"] = lin_w(H_DIM, sh)
    for k in "ifgo":
        out["W_x" + k + "_words"], out["W_x" + k + "_scales"] = lin_w(X_DIM, sx)
    return out


def reference(P, hidden, cell, ext_input,
              W_pi_words, W_pi_scales, b_pi, W_pf_words, W_pf_scales, b_pf,
              W_pg_words, W_pg_scales, b_pg, W_po_words, W_po_scales, b_po,
              W_hi_words, W_hi_scales, W_hf_words, W_hf_scales,
              W_hg_words, W_hg_scales, W_ho_words, W_ho_scales,
              W_xi_words, W_xi_scales, W_xf_words, W_xf_scales,
              W_xg_words, W_xg_scales, W_xo_words, W_xo_scales):
    Wp = np.concatenate([unpack_weight(W_pi_words, W_pi_scales, FMT).T, unpack_weight(W_pf_words, W_pf_scales, FMT).T,
                         unpack_weight(W_pg_words, W_pg_scales, FMT).T, unpack_weight(W_po_words, W_po_scales, FMT).T], axis=0)
    bp = np.concatenate([f64(b_pi), f64(b_pf), f64(b_pg), f64(b_po)], axis=0)
    Wh = np.concatenate([unpack_weight(W_hi_words, W_hi_scales, FMT).T, unpack_weight(W_hf_words, W_hf_scales, FMT).T,
                         unpack_weight(W_hg_words, W_hg_scales, FMT).T, unpack_weight(W_ho_words, W_ho_scales, FMT).T], axis=0)
    Wx = np.concatenate([unpack_weight(W_xi_words, W_xi_scales, FMT).T, unpack_weight(W_xf_words, W_xf_scales, FMT).T,
                         unpack_weight(W_xg_words, W_xg_scales, FMT).T, unpack_weight(W_xo_words, W_xo_scales, FMT).T], axis=0)
    gates = ((mxq(f64(P), 1, "e4m3") @ Wp.T) + bp
             + (mxq(f64(hidden), 1, "e4m3") @ Wh.T)
             + (mxq(f64(ext_input), 1, "e4m3") @ Wx.T))
    gi, gf, gg, go = np.split(gates, 4, axis=-1)
    i = sigmoid(gi)
    f = sigmoid(gf)
    g = np.tanh(gg)
    o = sigmoid(go)
    c_new = f * f64(cell) + i * g
    h_new = o * np.tanh(c_new)
    return (h_new, c_new)

@@ -1,0 +1,165 @@
+from contextlib import ExitStack
+
+import concourse.mybir as mybir
+from concourse.masks import make_identity
+
+F32 = mybir.dt.float32
+BF16 = mybir.dt.bfloat16
+I32 = mybir.dt.int32
+U32 = mybir.dt.uint32
+U8 = mybir.dt.uint8
+FP8X4 = mybir.dt.float8_e4m3fn_x4
+ACT = mybir.ActivationFunctionType
+ALU = mybir.AluOpType
+
+PARTS = 128
+BATCH = 128
+HID = 512
+K_PASS = 512
+WORDS_PASS = K_PASS // 2
+P_PASSES, X_PASSES, H_PASSES = 16, 4, 1
+PASSES = P_PASSES + X_PASSES + H_PASSES
+CHUNK = 4
+WORD_BUFS = 12
+
+FLOPS = 2 * BATCH * PASSES * K_PASS * 4 * HID
+
+
+def tile_structuredlstmcell_k_kernel(
+    tc,
+    P, hidden, cell, ext_input,
+    W_pi_words, W_pi_scales, b_pi, W_pf_words, W_pf_scales, b_pf,
+    W_pg_words, W_pg_scales, b_pg, W_po_words, W_po_scales, b_po,
+    W_hi_words, W_hi_scales, W_hf_words, W_hf_scales,
+    W_hg_words, W_hg_scales, W_ho_words, W_ho_scales,
+    W_xi_words, W_xi_scales, W_xf_words, W_xf_scales,
+    W_xg_words, W_xg_scales, W_xo_words, W_xo_scales,
+    out_0, out_1,
+):
+    nc = tc.nc
+
+    sources = [(P, P_PASSES), (ext_input, X_PASSES), (hidden, H_PASSES)]
+    gates = [
+        (ACT.Sigmoid, b_pi, [(W_pi_words, W_pi_scales), (W_xi_words, W_xi_scales), (W_hi_words, W_hi_scales)]),
+        (ACT.Sigmoid, b_pf, [(W_pf_words, W_pf_scales), (W_xf_words, W_xf_scales), (W_hf_words, W_hf_scales)]),
+        (ACT.Tanh, b_pg, [(W_pg_words, W_pg_scales), (W_xg_words, W_xg_scales), (W_hg_words, W_hg_scales)]),
+        (ACT.Sigmoid, b_po, [(W_po_words, W_po_scales), (W_xo_words, W_xo_scales), (W_ho_words, W_ho_scales)]),
+    ]
+    chunks = []
+    passes_before = 0
+    for s, (source, source_passes) in enumerate(sources):
+        for first in range(0, source_passes, CHUNK):
+            chunks.append((s, first, min(CHUNK, source_passes - first), passes_before + first))
+        passes_before += source_passes
+
+    with ExitStack() as ctx:
+        keep = ctx.enter_context(tc.tile_pool(name="keep", bufs=1))
+        stage = ctx.enter_context(tc.tile_pool(name="stage", bufs=2))
+        stream = ctx.enter_context(tc.tile_pool(name="stream", bufs=WORD_BUFS))
+        flip_banks = ctx.enter_context(tc.psum_pool(name="flip_banks", bufs=4))
+        bias_banks = ctx.enter_context(tc.psum_pool(name="bias_banks", bufs=2))
+        gate_banks = ctx.enter_context(tc.psum_pool(name="gate_banks", bufs=2))
+
+        acts = keep.tile([BATCH, PASSES * K_PASS], BF16)
+        for s, first, n, g0 in chunks:
+            nc.sync.dma_start(
+                out=acts[:, g0 * K_PASS : (g0 + n) * K_PASS],
+                in_=sources[s][0][:, first * K_PASS : (first + n) * K_PASS],
+            )
+
+        bias_rows = keep.tile([PARTS, 4 * HID], BF16)
+        nc.vector.memset(bias_rows[:].bitcast(I32), 0)
+        ones = keep.tile([PARTS, BATCH], BF16)
+        nc.vector.memset(ones[:], 1.0)
+        for b, (func, bias, weights) in enumerate(gates):
+            nc.scalar.dma_start(out=bias_rows[0:1, b * HID : (b + 1) * HID], in_=bias.unsqueeze(0))
+        cell_sb = keep.tile([BATCH, HID], BF16)
+        nc.scalar.dma_start(out=cell_sb[:], in_=cell)
+        bias_sb = keep.tile([BATCH, 4 * HID], F32)
+        for b in range(4):
+            spread = bias_banks.tile([BATCH, HID], F32)
+            nc.tensor.matmul(
+                out=spread[:], lhsT=ones[:], rhs=bias_rows[:, b * HID : (b + 1) * HID], start=True, stop=True
+            )
+            nc.scalar.copy(out=bias_sb[:, b * HID : (b + 1) * HID], in_=spread[:])
+
+        planes = {}
+        for b in range(4):
+            for s, (source, source_passes) in enumerate(sources):
+                planes[(b, s)] = keep.tile(
+                    [PARTS, source_passes, HID], U8, align_bytes=64, name="plane_%d_%d" % (b, s)
+                )
+                nc.vector.memset(planes[(b, s)][:].bitcast(I32), 0)
+        for b, (func, bias, weights) in enumerate(gates):
+            for s, (words, scales) in enumerate(weights):
+                for r in range(4):
+                    nc.gpsimd.dma_start(
+                        out=planes[(b, s)][4 * b + r : PARTS : 32, :, :].bitcast(F32),
+                        in_=scales[:, r : 16 : 4, :].rearrange("g q n -> q g n").bitcast(F32),
+                    )
+
+        ident = keep.tile([PARTS, PARTS], F32)
+        make_identity(nc, ident[:])
+        act_words = acts[:].bitcast(F32)
+        act_codes = keep.tile([PARTS, PASSES * BATCH], U32, align_bytes=64)
+        act_scales = keep.tile([PARTS, PASSES * BATCH], U8, align_bytes=64)
+        for s, first, n, g0 in chunks:
+            grouped = stage.tile([PARTS, n, BATCH, 4], BF16, align_bytes=64, tag="grouped")
+            grouped_words = grouped[:].bitcast(F32)
+            for j in range(n):
+                flipped = flip_banks.tile([PARTS, 2, BATCH], F32)
+                for u in range(2):
+                    nc.tensor.transpose(
+                        out=flipped[:, u, :],
+                        in_=act_words[:, (g0 + j) * WORDS_PASS + u : (g0 + j + 1) * WORDS_PASS : 2],
+                        identity=ident[:],
+                    )
+                nc.scalar.copy(out=grouped_words[:, j, :, :], in_=flipped[:].rearrange("p u m -> p m u"))
+            nc.vector.quantize_mx(
+                out=act_codes[:, g0 * BATCH : (g0 + n) * BATCH].bitcast(FP8X4),
+                scales=act_scales[:, g0 * BATCH : (g0 + n) * BATCH],
+                in_=grouped[:].rearrange("p g m t -> p (g m t)"),
+            )
+
+        def gate(b):
+            func, bias, weights = gates[b]
+            acc = gate_banks.tile([BATCH, HID], F32)
+            for s, first, n, g0 in chunks:
+                words = stream.tile([PARTS, n, 4 * HID], U8, align_bytes=64, tag="words")
+                nc.sync.dma_start(
+                    out=words[:].bitcast(I32),
+                    in_=weights[s][0][first : first + n].rearrange("g p n t -> p g (n t)").bitcast(I32),
+                )
+                for j in range(n):
+                    g = g0 + j
+                    nc.tensor.matmul_mx(
+                        out=acc[:],
+                        lhsT=act_codes[:, g * BATCH : (g + 1) * BATCH].bitcast(FP8X4),
+                        lhsT_scale=act_scales[:, g * BATCH : (g + 1) * BATCH],
+                        rhs=words[:, j, :].bitcast(FP8X4),
+                        rhs_scale=planes[(b, s)][4 * b : PARTS, first + j, :],
+                        start=(g == 0),
+                        stop=(g == PASSES - 1),
+                    )
+            biased = stage.tile([BATCH, HID], F32)
+            nc.vector.tensor_tensor(out=biased[:], in0=acc[:], in1=bias_sb[:, b * HID : (b + 1) * HID], op=ALU.add)
+            value = keep.tile([BATCH, HID], F32, name="gate_value_%d" % b)
+            nc.scalar.activation(out=value[:], in_=biased[:], func=func)
+            return value
+
+        i_gate = gate(0)
+        f_gate = gate(1)
+        kept = keep.tile([BATCH, HID], F32)
+        nc.vector.tensor_tensor(out=kept[:], in0=f_gate[:], in1=cell_sb[:], op=ALU.mult)
+        g_gate = gate(2)
+        fresh = keep.tile([BATCH, HID], F32)
+        nc.vector.tensor_tensor(out=fresh[:], in0=i_gate[:], in1=g_gate[:], op=ALU.mult)
+        c_new = keep.tile([BATCH, HID], F32)
+        nc.vector.tensor_tensor(out=c_new[:], in0=kept[:], in1=fresh[:], op=ALU.add)
+        nc.scalar.dma_start(out=out_1, in_=c_new[:])
+        tanh_c = keep.tile([BATCH, HID], F32)
+        nc.scalar.activation(out=tanh_c[:], in_=c_new[:], func=ACT.Tanh)
+        o_gate = gate(3)
+        h_new = keep.tile([BATCH, HID], F32)
+        nc.vector.tensor_tensor(out=h_new[:], in0=o_gate[:], in1=tanh_c[:], op=ALU.mult)
+        nc.sync.dma_start(out=out_0, in_=h_new[:])

@@ -21,6 +21,9 @@ P_PASSES, X_PASSES, H_PASSES = 16, 4, 1
 PASSES = P_PASSES + X_PASSES + H_PASSES
 CHUNK = 4
 WORD_BUFS = 12
+ROWS_QUADRANT = 4
+P_SOURCE, X_SOURCE, H_SOURCE = 0, 1, 2
+assert P_PASSES // CHUNK == ROWS_QUADRANT
 
 FLOPS = 2 * BATCH * PASSES * K_PASS * 4 * HID
 
@@ -90,13 +93,16 @@ def tile_structuredlstmcell_k_kernel(
                     [PARTS, source_passes, HID], U8, align_bytes=64, name="plane_%d_%d" % (b, s)
                 )
                 nc.vector.memset(planes[(b, s)][:].bitcast(I32), 0)
-        for b, (func, bias, weights) in enumerate(gates):
-            for s, (words, scales) in enumerate(weights):
-                for r in range(4):
-                    nc.gpsimd.dma_start(
-                        out=planes[(b, s)][4 * b + r : PARTS : 32, :, :].bitcast(F32),
-                        in_=scales[:, r : 16 : 4, :].rearrange("g q n -> q g n").bitcast(F32),
-                    )
+
+        def load_scale_rows(queue, view, b, s, r):
+            queue.dma_start(
+                out=planes[(b, s)][4 * b + r : PARTS : 32, :, :].bitcast(view),
+                in_=gates[b][2][s][1][:, r : 16 : 4, :].rearrange("g q n -> q g n").bitcast(view),
+            )
+
+        for b in range(4):
+            for r in range(ROWS_QUADRANT):
+                load_scale_rows(nc.gpsimd, F32, b, P_SOURCE, r)
 
         ident = keep.tile([PARTS, PARTS], F32)
         make_identity(nc, ident[:])
@@ -130,6 +136,9 @@ def tile_structuredlstmcell_k_kernel(
                     out=words[:].bitcast(I32),
                     in_=weights[s][0][first : first + n].rearrange("g p n t -> p g (n t)").bitcast(I32),
                 )
+                if s == P_SOURCE:
+                    for small in (X_SOURCE, H_SOURCE):
+                        load_scale_rows(nc.sync, I32, b, small, first // CHUNK)
                 for j in range(n):
                     g = g0 + j
                     nc.tensor.matmul_mx(

@@ -23,7 +23,7 @@ CHUNK = 4
 WORD_BUFS = 12
 ROWS_QUADRANT = 4
 P_SOURCE, X_SOURCE, H_SOURCE = 0, 1, 2
-assert P_PASSES // CHUNK == ROWS_QUADRANT
+HALF = HID // 2
 
 FLOPS = 2 * BATCH * PASSES * K_PASS * 4 * HID
 
@@ -87,22 +87,23 @@ def tile_structuredlstmcell_k_kernel(
             nc.scalar.copy(out=bias_sb[:, b * HID : (b + 1) * HID], in_=spread[:])
 
         planes = {}
-        for b in range(4):
-            for s, (source, source_passes) in enumerate(sources):
-                planes[(b, s)] = keep.tile(
-                    [PARTS, source_passes, HID], U8, align_bytes=64, name="plane_%d_%d" % (b, s)
-                )
-                nc.vector.memset(planes[(b, s)][:].bitcast(I32), 0)
 
-        def load_scale_rows(queue, view, b, s, r):
-            queue.dma_start(
-                out=planes[(b, s)][4 * b + r : PARTS : 32, :, :].bitcast(view),
-                in_=gates[b][2][s][1][:, r : 16 : 4, :].rearrange("g q n -> q g n").bitcast(view),
+        def load_plane(queue, b, s):
+            planes[(b, s)] = keep.tile(
+                [PARTS, sources[s][1], HID], U8, align_bytes=64, name="plane_%d_%d" % (b, s)
             )
+            nc.vector.memset(planes[(b, s)][:].bitcast(I32), 0)
+            for r in range(ROWS_QUADRANT):
+                queue.dma_start(
+                    out=planes[(b, s)][4 * b + r : PARTS : 32, :, :].bitcast(F32),
+                    in_=gates[b][2][s][1][:, r : 16 : 4, :].rearrange("g q n -> q g n").bitcast(F32),
+                )
 
         for b in range(4):
-            for r in range(ROWS_QUADRANT):
-                load_scale_rows(nc.gpsimd, F32, b, P_SOURCE, r)
+            load_plane(nc.scalar, b, H_SOURCE)
+        for b in range(4):
+            load_plane(nc.gpsimd, b, P_SOURCE)
+            load_plane(nc.gpsimd, b, X_SOURCE)
 
         ident = keep.tile([PARTS, PARTS], F32)
         make_identity(nc, ident[:])
@@ -127,6 +128,8 @@ def tile_structuredlstmcell_k_kernel(
                 in_=grouped[:].rearrange("p g m t -> p (g m t)"),
             )
 
+        halves = [slice(0, HALF), slice(HALF, HID)]
+
         def gate(b):
             func, bias, weights = gates[b]
             acc = gate_banks.tile([BATCH, HID], F32)
@@ -136,9 +139,6 @@ def tile_structuredlstmcell_k_kernel(
                     out=words[:].bitcast(I32),
                     in_=weights[s][0][first : first + n].rearrange("g p n t -> p g (n t)").bitcast(I32),
                 )
-                if s == P_SOURCE:
-                    for small in (X_SOURCE, H_SOURCE):
-                        load_scale_rows(nc.sync, I32, b, small, first // CHUNK)
                 for j in range(n):
                     g = g0 + j
                     nc.tensor.matmul_mx(
@@ -151,9 +151,12 @@ def tile_structuredlstmcell_k_kernel(
                         stop=(g == PASSES - 1),
                     )
             biased = stage.tile([BATCH, HID], F32)
-            nc.vector.tensor_tensor(out=biased[:], in0=acc[:], in1=bias_sb[:, b * HID : (b + 1) * HID], op=ALU.add)
             value = keep.tile([BATCH, HID], F32, name="gate_value_%d" % b)
-            nc.scalar.activation(out=value[:], in_=biased[:], func=func)
+            for half in halves:
+                nc.vector.tensor_tensor(
+                    out=biased[:, half], in0=acc[:, half], in1=bias_sb[:, b * HID : (b + 1) * HID][:, half], op=ALU.add
+                )
+                nc.scalar.activation(out=value[:, half], in_=biased[:, half], func=func)
             return value
 
         i_gate = gate(0)
@@ -170,5 +173,6 @@ def tile_structuredlstmcell_k_kernel(
         nc.scalar.activation(out=tanh_c[:], in_=c_new[:], func=ACT.Tanh)
         o_gate = gate(3)
         h_new = keep.tile([BATCH, HID], F32)
-        nc.vector.tensor_tensor(out=h_new[:], in0=o_gate[:], in1=tanh_c[:], op=ALU.mult)
-        nc.sync.dma_start(out=out_0, in_=h_new[:])
+        for half in halves:
+            nc.vector.tensor_tensor(out=h_new[:, half], in0=o_gate[:, half], in1=tanh_c[:, half], op=ALU.mult)
+            nc.sync.dma_start(out=out_0[:, half], in_=h_new[:, half])

@@ -56,12 +56,16 @@ def tile_structuredlstmcell_k_kernel(
         passes_before += source_passes
 
     with ExitStack() as ctx:
+        ctx.enter_context(tc.manual_schedule(engines={mybir.EngineType.SP, mybir.EngineType.Pool}))
         keep = ctx.enter_context(tc.tile_pool(name="keep", bufs=1))
         stage = ctx.enter_context(tc.tile_pool(name="stage", bufs=2))
         stream = ctx.enter_context(tc.tile_pool(name="stream", bufs=WORD_BUFS))
         flip_banks = ctx.enter_context(tc.psum_pool(name="flip_banks", bufs=4))
         bias_banks = ctx.enter_context(tc.psum_pool(name="bias_banks", bufs=2))
         gate_banks = ctx.enter_context(tc.psum_pool(name="gate_banks", bufs=2))
+
+        ident = keep.tile([PARTS, PARTS], F32)
+        make_identity(nc, ident[:])
 
         acts = keep.tile([BATCH, PASSES * K_PASS], BF16)
         for s, first, n, g0 in chunks:
@@ -88,25 +92,32 @@ def tile_structuredlstmcell_k_kernel(
 
         planes = {}
 
-        def load_plane(queue, b, s):
+        def make_plane(b, s):
             planes[(b, s)] = keep.tile(
                 [PARTS, sources[s][1], HID], U8, align_bytes=64, name="plane_%d_%d" % (b, s)
             )
             nc.vector.memset(planes[(b, s)][:].bitcast(I32), 0)
+
+        def load_plane_row(queue, b, s, r):
+            queue.dma_start(
+                out=planes[(b, s)][4 * b + r : PARTS : 32, :, :].bitcast(F32),
+                in_=gates[b][2][s][1][:, r : 16 : 4, :].rearrange("g q n -> q g n").bitcast(F32),
+            )
+
+        make_plane(0, P_SOURCE)
+        for b in range(4):
+            make_plane(b, H_SOURCE)
             for r in range(ROWS_QUADRANT):
-                queue.dma_start(
-                    out=planes[(b, s)][4 * b + r : PARTS : 32, :, :].bitcast(F32),
-                    in_=gates[b][2][s][1][:, r : 16 : 4, :].rearrange("g q n -> q g n").bitcast(F32),
-                )
-
+                load_plane_row(nc.scalar, b, H_SOURCE, r)
         for b in range(4):
-            load_plane(nc.scalar, b, H_SOURCE)
-        for b in range(4):
-            load_plane(nc.gpsimd, b, P_SOURCE)
-            load_plane(nc.gpsimd, b, X_SOURCE)
+            make_plane(b, X_SOURCE)
+            for r in range(ROWS_QUADRANT):
+                load_plane_row(nc.sync, b, X_SOURCE, r)
+        for b in range(1, 4):
+            make_plane(b, P_SOURCE)
+        for r in range(ROWS_QUADRANT):
+            load_plane_row(nc.gpsimd, 0, P_SOURCE, r)
 
-        ident = keep.tile([PARTS, PARTS], F32)
-        make_identity(nc, ident[:])
         act_words = acts[:].bitcast(F32)
         act_codes = keep.tile([PARTS, PASSES * BATCH], U32, align_bytes=64)
         act_scales = keep.tile([PARTS, PASSES * BATCH], U8, align_bytes=64)
@@ -133,12 +144,14 @@ def tile_structuredlstmcell_k_kernel(
         def gate(b):
             func, bias, weights = gates[b]
             acc = gate_banks.tile([BATCH, HID], F32)
-            for s, first, n, g0 in chunks:
+            for c, (s, first, n, g0) in enumerate(chunks):
                 words = stream.tile([PARTS, n, 4 * HID], U8, align_bytes=64, tag="words")
-                nc.sync.dma_start(
-                    out=words[:].bitcast(I32),
-                    in_=weights[s][0][first : first + n].rearrange("g p n t -> p g (n t)").bitcast(I32),
+                nc.gpsimd.dma_start(
+                    out=words[:].bitcast(F32),
+                    in_=weights[s][0][first : first + n].rearrange("g p n t -> p g (n t)").bitcast(F32),
                 )
+                if b < 3 and 1 <= c <= ROWS_QUADRANT:
+                    load_plane_row(nc.gpsimd, b + 1, P_SOURCE, c - 1)
                 for j in range(n):
                     g = g0 + j
                     nc.tensor.matmul_mx(

@@ -115,8 +115,15 @@ def tile_structuredlstmcell_k_kernel(
                 load_plane_row(nc.sync, b, X_SOURCE, r)
         for b in range(1, 4):
             make_plane(b, P_SOURCE)
-        for r in range(ROWS_QUADRANT):
-            load_plane_row(nc.gpsimd, 0, P_SOURCE, r)
+        for b in range(4):
+            for r in range(ROWS_QUADRANT):
+                for quadrant in (0, 2, 1, 3):
+                    q = 4 * quadrant + r
+                    p = 32 * quadrant + 4 * b + r
+                    nc.gpsimd.dma_start(
+                        out=planes[(b, P_SOURCE)][p : p + 1, :, :].bitcast(F32),
+                        in_=gates[b][2][P_SOURCE][1][:, q : q + 1, :].rearrange("g q n -> q g n").bitcast(F32),
+                    )
 
         act_words = acts[:].bitcast(F32)
         act_codes = keep.tile([PARTS, PASSES * BATCH], U32, align_bytes=64)
@@ -144,14 +151,12 @@ def tile_structuredlstmcell_k_kernel(
         def gate(b):
             func, bias, weights = gates[b]
             acc = gate_banks.tile([BATCH, HID], F32)
-            for c, (s, first, n, g0) in enumerate(chunks):
+            for s, first, n, g0 in chunks:
                 words = stream.tile([PARTS, n, 4 * HID], U8, align_bytes=64, tag="words")
-                nc.gpsimd.dma_start(
-                    out=words[:].bitcast(F32),
-                    in_=weights[s][0][first : first + n].rearrange("g p n t -> p g (n t)").bitcast(F32),
+                nc.sync.dma_start(
+                    out=words[:].bitcast(I32),
+                    in_=weights[s][0][first : first + n].rearrange("g p n t -> p g (n t)").bitcast(I32),
                 )
-                if b < 3 and 1 <= c <= ROWS_QUADRANT:
-                    load_plane_row(nc.gpsimd, b + 1, P_SOURCE, c - 1)
                 for j in range(n):
                     g = g0 + j
                     nc.tensor.matmul_mx(

@@ -148,10 +148,14 @@ def tile_structuredlstmcell_k_kernel(
 
         halves = [slice(0, HALF), slice(HALF, HID)]
 
+        fine_end = [chunk for chunk in chunks if chunk[0] == P_SOURCE]
+        fine_end.extend([(X_SOURCE, first, 1, P_PASSES + first) for first in range(X_PASSES)])
+        fine_end.append((H_SOURCE, 0, 1, P_PASSES + X_PASSES))
+
         def gate(b):
             func, bias, weights = gates[b]
             acc = gate_banks.tile([BATCH, HID], F32)
-            for s, first, n, g0 in chunks:
+            for s, first, n, g0 in fine_end if b == 3 else chunks:
                 words = stream.tile([PARTS, n, 4 * HID], U8, align_bytes=64, tag="words")
                 nc.sync.dma_start(
                     out=words[:].bitcast(I32),
@@ -186,10 +190,10 @@ def tile_structuredlstmcell_k_kernel(
         nc.vector.tensor_tensor(out=fresh[:], in0=i_gate[:], in1=g_gate[:], op=ALU.mult)
         c_new = keep.tile([BATCH, HID], F32)
         nc.vector.tensor_tensor(out=c_new[:], in0=kept[:], in1=fresh[:], op=ALU.add)
-        nc.scalar.dma_start(out=out_1, in_=c_new[:])
         tanh_c = keep.tile([BATCH, HID], F32)
         nc.scalar.activation(out=tanh_c[:], in_=c_new[:], func=ACT.Tanh)
         o_gate = gate(3)
+        nc.sync.dma_start(out=out_1, in_=c_new[:])
         h_new = keep.tile([BATCH, HID], F32)
         for half in halves:
             nc.vector.tensor_tensor(out=h_new[:, half], in0=o_gate[:, half], in1=tanh_c[:, half], op=ALU.mult)

@@ -115,7 +115,7 @@ def tile_structuredlstmcell_k_kernel(
                 load_plane_row(nc.sync, b, X_SOURCE, r)
         for b in range(1, 4):
             make_plane(b, P_SOURCE)
-        for b in range(4):
+        for b in range(3):
             for r in range(ROWS_QUADRANT):
                 for quadrant in (0, 2, 1, 3):
                     q = 4 * quadrant + r
@@ -124,6 +124,8 @@ def tile_structuredlstmcell_k_kernel(
                         out=planes[(b, P_SOURCE)][p : p + 1, :, :].bitcast(F32),
                         in_=gates[b][2][P_SOURCE][1][:, q : q + 1, :].rearrange("g q n -> q g n").bitcast(F32),
                     )
+        for r in range(ROWS_QUADRANT):
+            load_plane_row(nc.gpsimd, 3, P_SOURCE, r)
 
         act_words = acts[:].bitcast(F32)
         act_codes = keep.tile([PARTS, PASSES * BATCH], U32, align_bytes=64)

@@ -24,6 +24,7 @@ WORD_BUFS = 12
 ROWS_QUADRANT = 4
 P_SOURCE, X_SOURCE, H_SOURCE = 0, 1, 2
 HALF = HID // 2
+DMA_ALIGN = 256
 
 FLOPS = 2 * BATCH * PASSES * K_PASS * 4 * HID
 
@@ -67,20 +68,20 @@ def tile_structuredlstmcell_k_kernel(
         ident = keep.tile([PARTS, PARTS], F32)
         make_identity(nc, ident[:])
 
-        acts = keep.tile([BATCH, PASSES * K_PASS], BF16)
+        acts = keep.tile([BATCH, PASSES * K_PASS], BF16, align_bytes=DMA_ALIGN)
         for s, first, n, g0 in chunks:
             nc.sync.dma_start(
                 out=acts[:, g0 * K_PASS : (g0 + n) * K_PASS],
                 in_=sources[s][0][:, first * K_PASS : (first + n) * K_PASS],
             )
 
-        bias_rows = keep.tile([PARTS, 4 * HID], BF16)
+        bias_rows = keep.tile([PARTS, 4 * HID], BF16, align_bytes=DMA_ALIGN)
         nc.vector.memset(bias_rows[:].bitcast(I32), 0)
         ones = keep.tile([PARTS, BATCH], BF16)
         nc.vector.memset(ones[:], 1.0)
         for b, (func, bias, weights) in enumerate(gates):
             nc.scalar.dma_start(out=bias_rows[0:1, b * HID : (b + 1) * HID], in_=bias.unsqueeze(0))
-        cell_sb = keep.tile([BATCH, HID], BF16)
+        cell_sb = keep.tile([BATCH, HID], BF16, align_bytes=DMA_ALIGN)
         nc.scalar.dma_start(out=cell_sb[:], in_=cell)
         bias_sb = keep.tile([BATCH, 4 * HID], F32)
         for b in range(4):
@@ -94,7 +95,7 @@ def tile_structuredlstmcell_k_kernel(
 
         def make_plane(b, s):
             planes[(b, s)] = keep.tile(
-                [PARTS, sources[s][1], HID], U8, align_bytes=64, name="plane_%d_%d" % (b, s)
+                [PARTS, sources[s][1], HID], U8, align_bytes=DMA_ALIGN, name="plane_%d_%d" % (b, s)
             )
             nc.vector.memset(planes[(b, s)][:].bitcast(I32), 0)
 
@@ -158,7 +159,7 @@ def tile_structuredlstmcell_k_kernel(
             func, bias, weights = gates[b]
             acc = gate_banks.tile([BATCH, HID], F32)
             for s, first, n, g0 in fine_end if b == 3 else chunks:
-                words = stream.tile([PARTS, n, 4 * HID], U8, align_bytes=64, tag="words")
+                words = stream.tile([PARTS, n, 4 * HID], U8, align_bytes=DMA_ALIGN, tag="words")
                 nc.sync.dma_start(
                     out=words[:].bitcast(I32),
                     in_=weights[s][0][first : first + n].rearrange("g p n t -> p g (n t)").bitcast(I32),
@@ -190,13 +191,13 @@ def tile_structuredlstmcell_k_kernel(
         g_gate = gate(2)
         fresh = keep.tile([BATCH, HID], F32)
         nc.vector.tensor_tensor(out=fresh[:], in0=i_gate[:], in1=g_gate[:], op=ALU.mult)
-        c_new = keep.tile([BATCH, HID], F32)
+        c_new = keep.tile([BATCH, HID], F32, align_bytes=DMA_ALIGN)
         nc.vector.tensor_tensor(out=c_new[:], in0=kept[:], in1=fresh[:], op=ALU.add)
         tanh_c = keep.tile([BATCH, HID], F32)
         nc.scalar.activation(out=tanh_c[:], in_=c_new[:], func=ACT.Tanh)
         o_gate = gate(3)
         nc.sync.dma_start(out=out_1, in_=c_new[:])
-        h_new = keep.tile([BATCH, HID], F32)
+        h_new = keep.tile([BATCH, HID], F32, align_bytes=DMA_ALIGN)
         for half in halves:
             nc.vector.tensor_tensor(out=h_new[:, half], in0=o_gate[:, half], in1=tanh_c[:, half], op=ALU.mult)
             nc.sync.dma_start(out=out_0[:, half], in_=h_new[:, half])

@@ -20,7 +20,8 @@ WORDS_PASS = K_PASS // 2
 P_PASSES, X_PASSES, H_PASSES = 16, 4, 1
 PASSES = P_PASSES + X_PASSES + H_PASSES
 CHUNK = 4
-WORD_BUFS = 12
+WORD_CHUNK = 8
+WORD_BUFS = 6
 ROWS_QUADRANT = 4
 P_SOURCE, X_SOURCE, H_SOURCE = 0, 1, 2
 HALF = HID // 2
@@ -49,12 +50,17 @@ def tile_structuredlstmcell_k_kernel(
         (ACT.Tanh, b_pg, [(W_pg_words, W_pg_scales), (W_xg_words, W_xg_scales), (W_hg_words, W_hg_scales)]),
         (ACT.Sigmoid, b_po, [(W_po_words, W_po_scales), (W_xo_words, W_xo_scales), (W_ho_words, W_ho_scales)]),
     ]
-    chunks = []
-    passes_before = 0
-    for s, (source, source_passes) in enumerate(sources):
-        for first in range(0, source_passes, CHUNK):
-            chunks.append((s, first, min(CHUNK, source_passes - first), passes_before + first))
-        passes_before += source_passes
+    def cut(most):
+        pieces = []
+        passes_before = 0
+        for s, (source, source_passes) in enumerate(sources):
+            for first in range(0, source_passes, most):
+                pieces.append((s, first, min(most, source_passes - first), passes_before + first))
+            passes_before += source_passes
+        return pieces
+
+    chunks = cut(CHUNK)
+    word_chunks = cut(WORD_CHUNK)
 
     with ExitStack() as ctx:
         ctx.enter_context(tc.manual_schedule(engines={mybir.EngineType.SP, mybir.EngineType.Pool}))
@@ -94,9 +100,8 @@ def tile_structuredlstmcell_k_kernel(
         planes = {}
 
         def make_plane(b, s):
-            planes[(b, s)] = keep.tile(
-                [PARTS, sources[s][1], HID], U8, align_bytes=DMA_ALIGN, name="plane_%d_%d" % (b, s)
-            )
+            blocks = 1 if s == X_SOURCE else sources[s][1]
+            planes[(b, s)] = keep.tile([PARTS, blocks, HID], U8, align_bytes=DMA_ALIGN, name="plane_%d_%d" % (b, s))
             nc.vector.memset(planes[(b, s)][:].bitcast(I32), 0)
 
         def load_plane_row(queue, b, s, r):
@@ -105,17 +110,25 @@ def tile_structuredlstmcell_k_kernel(
                 in_=gates[b][2][s][1][:, r : 16 : 4, :].rearrange("g q n -> q g n").bitcast(F32),
             )
 
+        def load_x_quadrant(b, quadrant):
+            nc.sync.dma_start(
+                out=planes[(b, X_SOURCE)][32 * quadrant : 32 * quadrant + 16, 0, :].bitcast(I32),
+                in_=gates[b][2][X_SOURCE][1][:, 4 * quadrant : 4 * quadrant + 4, :].bitcast(I32),
+            )
+
+        def load_h_row(b, r):
+            nc.sync.dma_start(
+                out=planes[(b, H_SOURCE)][r : PARTS : 32, 0, :].bitcast(I32),
+                in_=gates[b][2][H_SOURCE][1][0, r : 16 : 4, :].bitcast(I32),
+            )
+
         make_plane(0, P_SOURCE)
-        for b in range(4):
-            make_plane(b, H_SOURCE)
-            for r in range(ROWS_QUADRANT):
-                load_plane_row(nc.scalar, b, H_SOURCE, r)
-        for b in range(4):
-            make_plane(b, X_SOURCE)
-            for r in range(ROWS_QUADRANT):
-                load_plane_row(nc.sync, b, X_SOURCE, r)
+        make_plane(0, X_SOURCE)
+        make_plane(0, H_SOURCE)
         for b in range(1, 4):
             make_plane(b, P_SOURCE)
+            make_plane(b, X_SOURCE)
+            make_plane(b, H_SOURCE)
         for b in range(3):
             for r in range(ROWS_QUADRANT):
                 for quadrant in (0, 2, 1, 3):
@@ -151,27 +164,39 @@ def tile_structuredlstmcell_k_kernel(
 
         halves = [slice(0, HALF), slice(HALF, HID)]
 
-        fine_end = [chunk for chunk in chunks if chunk[0] == P_SOURCE]
+        fine_end = [chunk for chunk in word_chunks if chunk[0] == P_SOURCE]
         fine_end.extend([(X_SOURCE, first, 1, P_PASSES + first) for first in range(X_PASSES)])
         fine_end.append((H_SOURCE, 0, 1, P_PASSES + X_PASSES))
 
         def gate(b):
             func, bias, weights = gates[b]
             acc = gate_banks.tile([BATCH, HID], F32)
-            for s, first, n, g0 in fine_end if b == 3 else chunks:
+            for s, first, n, g0 in fine_end if b == 3 else word_chunks:
                 words = stream.tile([PARTS, n, 4 * HID], U8, align_bytes=DMA_ALIGN, tag="words")
                 nc.sync.dma_start(
                     out=words[:].bitcast(I32),
                     in_=weights[s][0][first : first + n].rearrange("g p n t -> p g (n t)").bitcast(I32),
                 )
+                if s == P_SOURCE:
+                    for i in range(4):
+                        if first == 0:
+                            load_x_quadrant(b, i)
+                        else:
+                            load_h_row(b, i)
                 for j in range(n):
                     g = g0 + j
+                    if s == P_SOURCE:
+                        row, block = 4 * b, first + j
+                    elif s == X_SOURCE:
+                        row, block = 4 * (first + j), 0
+                    else:
+                        row, block = 0, 0
                     nc.tensor.matmul_mx(
                         out=acc[:],
                         lhsT=act_codes[:, g * BATCH : (g + 1) * BATCH].bitcast(FP8X4),
                         lhsT_scale=act_scales[:, g * BATCH : (g + 1) * BATCH],
                         rhs=words[:, j, :].bitcast(FP8X4),
-                        rhs_scale=planes[(b, s)][4 * b : PARTS, first + j, :],
+                        rhs_scale=planes[(b, s)][row:PARTS, block, :],
                         start=(g == 0),
                         stop=(g == PASSES - 1),
                     )

@@ -104,10 +104,13 @@ def tile_structuredlstmcell_k_kernel(
             planes[(b, s)] = keep.tile([PARTS, blocks, HID], U8, align_bytes=DMA_ALIGN, name="plane_%d_%d" % (b, s))
             nc.vector.memset(planes[(b, s)][:].bitcast(I32), 0)
 
-        def load_plane_row(queue, b, s, r):
+        def load_p_partition(queue, dtype, b, i):
+            r, quadrant = i // 4, (0, 2, 1, 3)[i % 4]
+            q = 4 * quadrant + r
+            p = 32 * quadrant + 4 * b + r
             queue.dma_start(
-                out=planes[(b, s)][4 * b + r : PARTS : 32, :, :].bitcast(F32),
-                in_=gates[b][2][s][1][:, r : 16 : 4, :].rearrange("g q n -> q g n").bitcast(F32),
+                out=planes[(b, P_SOURCE)][p : p + 1, :, :].bitcast(dtype),
+                in_=gates[b][2][P_SOURCE][1][:, q : q + 1, :].rearrange("g q n -> q g n").bitcast(dtype),
             )
 
         def load_x_quadrant(b, quadrant):
@@ -130,16 +133,9 @@ def tile_structuredlstmcell_k_kernel(
             make_plane(b, X_SOURCE)
             make_plane(b, H_SOURCE)
         for b in range(3):
-            for r in range(ROWS_QUADRANT):
-                for quadrant in (0, 2, 1, 3):
-                    q = 4 * quadrant + r
-                    p = 32 * quadrant + 4 * b + r
-                    nc.gpsimd.dma_start(
-                        out=planes[(b, P_SOURCE)][p : p + 1, :, :].bitcast(F32),
-                        in_=gates[b][2][P_SOURCE][1][:, q : q + 1, :].rearrange("g q n -> q g n").bitcast(F32),
-                    )
-        for r in range(ROWS_QUADRANT):
-            load_plane_row(nc.gpsimd, 3, P_SOURCE, r)
+            for i in range(16):
+                load_p_partition(nc.gpsimd, F32, b, i)
+        late_rows = list(range(16))
 
         act_words = acts[:].bitcast(F32)
         act_codes = keep.tile([PARTS, PASSES * BATCH], U32, align_bytes=64)
@@ -183,6 +179,12 @@ def tile_structuredlstmcell_k_kernel(
                             load_x_quadrant(b, i)
                         else:
                             load_h_row(b, i)
+                if b < 3:
+                    for more in range({(P_SOURCE, 0): 2, (P_SOURCE, 8): 2, (X_SOURCE, 0): 2}.get((s, first), 0)):
+                        if len(late_rows) > 0:
+                            i = late_rows[0]
+                            late_rows.remove(i)
+                            load_p_partition(nc.sync, I32, 3, i)
                 for j in range(n):
                     g = g0 + j
                     if s == P_SOURCE:

@@ -20,8 +20,11 @@ WORDS_PASS = K_PASS // 2
 P_PASSES, X_PASSES, H_PASSES = 16, 4, 1
 PASSES = P_PASSES + X_PASSES + H_PASSES
 CHUNK = 4
+ACT_CHUNK = 8
 WORD_CHUNK = 8
-WORD_BUFS = 6
+LAST_CHUNK = 2
+P_BUFS = 5
+BUFS = 2
 ROWS_QUADRANT = 4
 P_SOURCE, X_SOURCE, H_SOURCE = 0, 1, 2
 HALF = HID // 2
@@ -66,20 +69,13 @@ def tile_structuredlstmcell_k_kernel(
         ctx.enter_context(tc.manual_schedule(engines={mybir.EngineType.SP, mybir.EngineType.Pool}))
         keep = ctx.enter_context(tc.tile_pool(name="keep", bufs=1))
         stage = ctx.enter_context(tc.tile_pool(name="stage", bufs=2))
-        stream = ctx.enter_context(tc.tile_pool(name="stream", bufs=WORD_BUFS))
+        stream = ctx.enter_context(tc.tile_pool(name="stream", bufs=BUFS))
         flip_banks = ctx.enter_context(tc.psum_pool(name="flip_banks", bufs=4))
         bias_banks = ctx.enter_context(tc.psum_pool(name="bias_banks", bufs=2))
         gate_banks = ctx.enter_context(tc.psum_pool(name="gate_banks", bufs=2))
 
         ident = keep.tile([PARTS, PARTS], F32)
         make_identity(nc, ident[:])
-
-        acts = keep.tile([BATCH, PASSES * K_PASS], BF16, align_bytes=DMA_ALIGN)
-        for s, first, n, g0 in chunks:
-            nc.sync.dma_start(
-                out=acts[:, g0 * K_PASS : (g0 + n) * K_PASS],
-                in_=sources[s][0][:, first * K_PASS : (first + n) * K_PASS],
-            )
 
         bias_rows = keep.tile([PARTS, 4 * HID], BF16, align_bytes=DMA_ALIGN)
         nc.vector.memset(bias_rows[:].bitcast(I32), 0)
@@ -89,6 +85,13 @@ def tile_structuredlstmcell_k_kernel(
             nc.scalar.dma_start(out=bias_rows[0:1, b * HID : (b + 1) * HID], in_=bias.unsqueeze(0))
         cell_sb = keep.tile([BATCH, HID], BF16, align_bytes=DMA_ALIGN)
         nc.scalar.dma_start(out=cell_sb[:], in_=cell)
+        acts = keep.tile([BATCH, PASSES * K_PASS], BF16, align_bytes=DMA_ALIGN)
+        for s, first, n, g0 in cut(ACT_CHUNK):
+            nc.sync.dma_start(
+                out=acts[:, g0 * K_PASS : (g0 + n) * K_PASS],
+                in_=sources[s][0][:, first * K_PASS : (first + n) * K_PASS],
+            )
+
         bias_sb = keep.tile([BATCH, 4 * HID], F32)
         for b in range(4):
             spread = bias_banks.tile([BATCH, HID], F32)
@@ -132,10 +135,12 @@ def tile_structuredlstmcell_k_kernel(
             make_plane(b, P_SOURCE)
             make_plane(b, X_SOURCE)
             make_plane(b, H_SOURCE)
-        for b in range(3):
+        for b in range(2):
             for i in range(16):
                 load_p_partition(nc.gpsimd, F32, b, i)
-        late_rows = list(range(16))
+        for i in range(8):
+            load_p_partition(nc.gpsimd, F32, 2, i)
+        late_rows = [(2, i) for i in range(8, 16)] + [(3, i) for i in range(16)]
 
         act_words = acts[:].bitcast(F32)
         act_codes = keep.tile([PARTS, PASSES * BATCH], U32, align_bytes=64)
@@ -161,14 +166,16 @@ def tile_structuredlstmcell_k_kernel(
         halves = [slice(0, HALF), slice(HALF, HID)]
 
         fine_end = [chunk for chunk in word_chunks if chunk[0] == P_SOURCE]
-        fine_end.extend([(X_SOURCE, first, 1, P_PASSES + first) for first in range(X_PASSES)])
+        fine_end.extend([(X_SOURCE, first, LAST_CHUNK, P_PASSES + first) for first in range(0, X_PASSES, LAST_CHUNK)])
         fine_end.append((H_SOURCE, 0, 1, P_PASSES + X_PASSES))
 
         def gate(b):
             func, bias, weights = gates[b]
             acc = gate_banks.tile([BATCH, HID], F32)
             for s, first, n, g0 in fine_end if b == 3 else word_chunks:
-                words = stream.tile([PARTS, n, 4 * HID], U8, align_bytes=DMA_ALIGN, tag="words")
+                words = stream.tile(
+                    [PARTS, n, 4 * HID], U8, align_bytes=DMA_ALIGN, tag="words_%d_%d" % (s, n), bufs=P_BUFS if s == P_SOURCE else BUFS
+                )
                 nc.sync.dma_start(
                     out=words[:].bitcast(I32),
                     in_=weights[s][0][first : first + n].rearrange("g p n t -> p g (n t)").bitcast(I32),
@@ -180,11 +187,11 @@ def tile_structuredlstmcell_k_kernel(
                         else:
                             load_h_row(b, i)
                 if b < 3:
-                    for more in range({(P_SOURCE, 0): 2, (P_SOURCE, 8): 2, (X_SOURCE, 0): 2}.get((s, first), 0)):
+                    for more in range({(P_SOURCE, 0): 2, (P_SOURCE, 8): 2, (X_SOURCE, 0): 4}.get((s, first), 0)):
                         if len(late_rows) > 0:
-                            i = late_rows[0]
-                            late_rows.remove(i)
-                            load_p_partition(nc.sync, I32, 3, i)
+                            late = late_rows[0]
+                            late_rows.remove(late)
+                            load_p_partition(nc.sync, I32, late[0], late[1])
                 for j in range(n):
                     g = g0 + j
                     if s == P_SOURCE:

@@ -22,8 +22,7 @@ PASSES = P_PASSES + X_PASSES + H_PASSES
 CHUNK = 4
 ACT_CHUNK = 8
 WORD_CHUNK = 8
-LAST_CHUNK = 2
-P_BUFS = 5
+P_BUFS = 6
 BUFS = 2
 ROWS_QUADRANT = 4
 P_SOURCE, X_SOURCE, H_SOURCE = 0, 1, 2
@@ -165,21 +164,22 @@ def tile_structuredlstmcell_k_kernel(
 
         halves = [slice(0, HALF), slice(HALF, HID)]
 
-        fine_end = [chunk for chunk in word_chunks if chunk[0] == P_SOURCE]
-        fine_end.extend([(X_SOURCE, first, LAST_CHUNK, P_PASSES + first) for first in range(0, X_PASSES, LAST_CHUNK)])
-        fine_end.append((H_SOURCE, 0, 1, P_PASSES + X_PASSES))
+        last_pieces = {(P_SOURCE, 0): [8], (P_SOURCE, 8): [4, 4], (X_SOURCE, 0): [1, 1, 1, 1], (H_SOURCE, 0): [1]}
 
         def gate(b):
             func, bias, weights = gates[b]
             acc = gate_banks.tile([BATCH, HID], F32)
-            for s, first, n, g0 in fine_end if b == 3 else word_chunks:
+            for s, first, n, g0 in word_chunks:
                 words = stream.tile(
-                    [PARTS, n, 4 * HID], U8, align_bytes=DMA_ALIGN, tag="words_%d_%d" % (s, n), bufs=P_BUFS if s == P_SOURCE else BUFS
+                    [PARTS, n, 4 * HID], U8, align_bytes=DMA_ALIGN, tag="words_%d" % s, bufs=P_BUFS if s == P_SOURCE else BUFS
                 )
-                nc.sync.dma_start(
-                    out=words[:].bitcast(I32),
-                    in_=weights[s][0][first : first + n].rearrange("g p n t -> p g (n t)").bitcast(I32),
-                )
+                at = 0
+                for piece in last_pieces[(s, first)] if b == 3 else [n]:
+                    nc.sync.dma_start(
+                        out=words[:, at : at + piece, :].bitcast(I32),
+                        in_=weights[s][0][first + at : first + at + piece].rearrange("g p n t -> p g (n t)").bitcast(I32),
+                    )
+                    at += piece
                 if s == P_SOURCE:
                     for i in range(4):
                         if first == 0:

from contextlib import ExitStack

import concourse.mybir as mybir
from concourse.masks import make_identity

F32 = mybir.dt.float32
BF16 = mybir.dt.bfloat16
I32 = mybir.dt.int32
U32 = mybir.dt.uint32
U8 = mybir.dt.uint8
FP8X4 = mybir.dt.float8_e4m3fn_x4
ACT = mybir.ActivationFunctionType
ALU = mybir.AluOpType

PARTS = 128
BATCH = 128
HID = 512
K_PASS = 512
WORDS_PASS = K_PASS // 2
P_PASSES, X_PASSES, H_PASSES = 16, 4, 1
PASSES = P_PASSES + X_PASSES + H_PASSES
CHUNK = 4
ACT_CHUNK = 8
WORD_CHUNK = 8
P_BUFS = 6
BUFS = 2
ROWS_QUADRANT = 4
P_SOURCE, X_SOURCE, H_SOURCE = 0, 1, 2
HALF = HID // 2
DMA_ALIGN = 256

FLOPS = 2 * BATCH * PASSES * K_PASS * 4 * HID


def tile_structuredlstmcell_k_kernel(
    tc,
    P, hidden, cell, ext_input,
    W_pi_words, W_pi_scales, b_pi, W_pf_words, W_pf_scales, b_pf,
    W_pg_words, W_pg_scales, b_pg, W_po_words, W_po_scales, b_po,
    W_hi_words, W_hi_scales, W_hf_words, W_hf_scales,
    W_hg_words, W_hg_scales, W_ho_words, W_ho_scales,
    W_xi_words, W_xi_scales, W_xf_words, W_xf_scales,
    W_xg_words, W_xg_scales, W_xo_words, W_xo_scales,
    out_0, out_1,
):
    nc = tc.nc

    sources = [(P, P_PASSES), (ext_input, X_PASSES), (hidden, H_PASSES)]
    gates = [
        (ACT.Sigmoid, b_pi, [(W_pi_words, W_pi_scales), (W_xi_words, W_xi_scales), (W_hi_words, W_hi_scales)]),
        (ACT.Sigmoid, b_pf, [(W_pf_words, W_pf_scales), (W_xf_words, W_xf_scales), (W_hf_words, W_hf_scales)]),
        (ACT.Tanh, b_pg, [(W_pg_words, W_pg_scales), (W_xg_words, W_xg_scales), (W_hg_words, W_hg_scales)]),
        (ACT.Sigmoid, b_po, [(W_po_words, W_po_scales), (W_xo_words, W_xo_scales), (W_ho_words, W_ho_scales)]),
    ]
    def cut(most):
        pieces = []
        passes_before = 0
        for s, (source, source_passes) in enumerate(sources):
            for first in range(0, source_passes, most):
                pieces.append((s, first, min(most, source_passes - first), passes_before + first))
            passes_before += source_passes
        return pieces

    chunks = cut(CHUNK)
    word_chunks = cut(WORD_CHUNK)

    with ExitStack() as ctx:
        ctx.enter_context(tc.manual_schedule(engines={mybir.EngineType.SP, mybir.EngineType.Pool}))
        keep = ctx.enter_context(tc.tile_pool(name="keep", bufs=1))
        stage = ctx.enter_context(tc.tile_pool(name="stage", bufs=2))
        stream = ctx.enter_context(tc.tile_pool(name="stream", bufs=BUFS))
        flip_banks = ctx.enter_context(tc.psum_pool(name="flip_banks", bufs=4))
        bias_banks = ctx.enter_context(tc.psum_pool(name="bias_banks", bufs=2))
        gate_banks = ctx.enter_context(tc.psum_pool(name="gate_banks", bufs=2))

        ident = keep.tile([PARTS, PARTS], F32)
        make_identity(nc, ident[:])

        bias_rows = keep.tile([PARTS, 4 * HID], BF16, align_bytes=DMA_ALIGN)
        nc.vector.memset(bias_rows[:].bitcast(I32), 0)
        ones = keep.tile([PARTS, BATCH], BF16)
        nc.vector.memset(ones[:], 1.0)
        for b, (func, bias, weights) in enumerate(gates):
            nc.scalar.dma_start(out=bias_rows[0:1, b * HID : (b + 1) * HID], in_=bias.unsqueeze(0))
        cell_sb = keep.tile([BATCH, HID], BF16, align_bytes=DMA_ALIGN)
        nc.scalar.dma_start(out=cell_sb[:], in_=cell)
        acts = keep.tile([BATCH, PASSES * K_PASS], BF16, align_bytes=DMA_ALIGN)
        for s, first, n, g0 in cut(ACT_CHUNK):
            nc.sync.dma_start(
                out=acts[:, g0 * K_PASS : (g0 + n) * K_PASS],
                in_=sources[s][0][:, first * K_PASS : (first + n) * K_PASS],
            )

        bias_sb = keep.tile([BATCH, 4 * HID], F32)
        for b in range(4):
            spread = bias_banks.tile([BATCH, HID], F32)
            nc.tensor.matmul(
                out=spread[:], lhsT=ones[:], rhs=bias_rows[:, b * HID : (b + 1) * HID], start=True, stop=True
            )
            nc.scalar.copy(out=bias_sb[:, b * HID : (b + 1) * HID], in_=spread[:])

        planes = {}

        def make_plane(b, s):
            blocks = 1 if s == X_SOURCE else sources[s][1]
            planes[(b, s)] = keep.tile([PARTS, blocks, HID], U8, align_bytes=DMA_ALIGN, name="plane_%d_%d" % (b, s))
            nc.vector.memset(planes[(b, s)][:].bitcast(I32), 0)

        def load_p_partition(queue, dtype, b, i):
            r, quadrant = i // 4, (0, 2, 1, 3)[i % 4]
            q = 4 * quadrant + r
            p = 32 * quadrant + 4 * b + r
            queue.dma_start(
                out=planes[(b, P_SOURCE)][p : p + 1, :, :].bitcast(dtype),
                in_=gates[b][2][P_SOURCE][1][:, q : q + 1, :].rearrange("g q n -> q g n").bitcast(dtype),
            )

        def load_x_quadrant(b, quadrant):
            nc.sync.dma_start(
                out=planes[(b, X_SOURCE)][32 * quadrant : 32 * quadrant + 16, 0, :].bitcast(I32),
                in_=gates[b][2][X_SOURCE][1][:, 4 * quadrant : 4 * quadrant + 4, :].bitcast(I32),
            )

        def load_h_row(b, r):
            nc.sync.dma_start(
                out=planes[(b, H_SOURCE)][r : PARTS : 32, 0, :].bitcast(I32),
                in_=gates[b][2][H_SOURCE][1][0, r : 16 : 4, :].bitcast(I32),
            )

        make_plane(0, P_SOURCE)
        make_plane(0, X_SOURCE)
        make_plane(0, H_SOURCE)
        for b in range(1, 4):
            make_plane(b, P_SOURCE)
            make_plane(b, X_SOURCE)
            make_plane(b, H_SOURCE)
        for b in range(2):
            for i in range(16):
                load_p_partition(nc.gpsimd, F32, b, i)
        for i in range(8):
            load_p_partition(nc.gpsimd, F32, 2, i)
        late_rows = [(2, i) for i in range(8, 16)] + [(3, i) for i in range(16)]

        act_words = acts[:].bitcast(F32)
        act_codes = keep.tile([PARTS, PASSES * BATCH], U32, align_bytes=64)
        act_scales = keep.tile([PARTS, PASSES * BATCH], U8, align_bytes=64)
        for s, first, n, g0 in chunks:
            grouped = stage.tile([PARTS, n, BATCH, 4], BF16, align_bytes=64, tag="grouped")
            grouped_words = grouped[:].bitcast(F32)
            for j in range(n):
                flipped = flip_banks.tile([PARTS, 2, BATCH], F32)
                for u in range(2):
                    nc.tensor.transpose(
                        out=flipped[:, u, :],
                        in_=act_words[:, (g0 + j) * WORDS_PASS + u : (g0 + j + 1) * WORDS_PASS : 2],
                        identity=ident[:],
                    )
                nc.scalar.copy(out=grouped_words[:, j, :, :], in_=flipped[:].rearrange("p u m -> p m u"))
            nc.vector.quantize_mx(
                out=act_codes[:, g0 * BATCH : (g0 + n) * BATCH].bitcast(FP8X4),
                scales=act_scales[:, g0 * BATCH : (g0 + n) * BATCH],
                in_=grouped[:].rearrange("p g m t -> p (g m t)"),
            )

        halves = [slice(0, HALF), slice(HALF, HID)]

        last_pieces = {(P_SOURCE, 0): [8], (P_SOURCE, 8): [4, 4], (X_SOURCE, 0): [1, 1, 1, 1], (H_SOURCE, 0): [1]}

        def gate(b):
            func, bias, weights = gates[b]
            acc = gate_banks.tile([BATCH, HID], F32)
            for s, first, n, g0 in word_chunks:
                words = stream.tile(
                    [PARTS, n, 4 * HID], U8, align_bytes=DMA_ALIGN, tag="words_%d" % s, bufs=P_BUFS if s == P_SOURCE else BUFS
                )
                at = 0
                for piece in last_pieces[(s, first)] if b == 3 else [n]:
                    nc.sync.dma_start(
                        out=words[:, at : at + piece, :].bitcast(I32),
                        in_=weights[s][0][first + at : first + at + piece].rearrange("g p n t -> p g (n t)").bitcast(I32),
                    )
                    at += piece
                if s == P_SOURCE:
                    for i in range(4):
                        if first == 0:
                            load_x_quadrant(b, i)
                        else:
                            load_h_row(b, i)
                if b < 3:
                    for more in range({(P_SOURCE, 0): 2, (P_SOURCE, 8): 2, (X_SOURCE, 0): 4}.get((s, first), 0)):
                        if len(late_rows) > 0:
                            late = late_rows[0]
                            late_rows.remove(late)
                            load_p_partition(nc.sync, I32, late[0], late[1])
                for j in range(n):
                    g = g0 + j
                    if s == P_SOURCE:
                        row, block = 4 * b, first + j
                    elif s == X_SOURCE:
                        row, block = 4 * (first + j), 0
                    else:
                        row, block = 0, 0
                    nc.tensor.matmul_mx(
                        out=acc[:],
                        lhsT=act_codes[:, g * BATCH : (g + 1) * BATCH].bitcast(FP8X4),
                        lhsT_scale=act_scales[:, g * BATCH : (g + 1) * BATCH],
                        rhs=words[:, j, :].bitcast(FP8X4),
                        rhs_scale=planes[(b, s)][row:PARTS, block, :],
                        start=(g == 0),
                        stop=(g == PASSES - 1),
                    )
            biased = stage.tile([BATCH, HID], F32)
            value = keep.tile([BATCH, HID], F32, name="gate_value_%d" % b)
            for half in halves:
                nc.vector.tensor_tensor(
                    out=biased[:, half], in0=acc[:, half], in1=bias_sb[:, b * HID : (b + 1) * HID][:, half], op=ALU.add
                )
                nc.scalar.activation(out=value[:, half], in_=biased[:, half], func=func)
            return value

        i_gate = gate(0)
        f_gate = gate(1)
        kept = keep.tile([BATCH, HID], F32)
        nc.vector.tensor_tensor(out=kept[:], in0=f_gate[:], in1=cell_sb[:], op=ALU.mult)
        g_gate = gate(2)
        fresh = keep.tile([BATCH, HID], F32)
        nc.vector.tensor_tensor(out=fresh[:], in0=i_gate[:], in1=g_gate[:], op=ALU.mult)
        c_new = keep.tile([BATCH, HID], F32, align_bytes=DMA_ALIGN)
        nc.vector.tensor_tensor(out=c_new[:], in0=kept[:], in1=fresh[:], op=ALU.add)
        tanh_c = keep.tile([BATCH, HID], F32)
        nc.scalar.activation(out=tanh_c[:], in_=c_new[:], func=ACT.Tanh)
        o_gate = gate(3)
        nc.sync.dma_start(out=out_1, in_=c_new[:])
        h_new = keep.tile([BATCH, HID], F32, align_bytes=DMA_ALIGN)
        for half in halves:
            nc.vector.tensor_tensor(out=h_new[:, half], in0=o_gate[:, half], in1=tanh_c[:, half], op=ALU.mult)
            nc.sync.dma_start(out=out_0[:, half], in_=h_new[:, half])
